import numpy as np
import ml_dtypes


def mxq(x, axis, fmt="e4m3"):
    dtype, down = {"e4m3": (ml_dtypes.float8_e4m3fn, 7), "e5m2": (ml_dtypes.float8_e5m2, 14)}[fmt]
    v = np.moveaxis(np.asarray(x, np.float32).astype(ml_dtypes.bfloat16).astype(np.float64), axis, -1)
    blocks = v.reshape(v.shape[:-1] + (-1, 32))
    amax = np.abs(blocks).max(-1, keepdims=True)
    byte = np.maximum(np.where(amax > 0, np.frexp(amax)[1] - 1 + 127, 0) - down, 1)
    scale = np.exp2(byte - 127.0)
    codes = (blocks / scale).astype(np.float32).astype(dtype).astype(np.float64)
    return np.moveaxis((codes * scale).reshape(v.shape), -1, axis)


WIDE = False


def mx_kscale(k):
    if not WIDE:
        return np.ones(k)
    levels = np.array([10, -10, 5, -5, 0])
    a = np.random.permutation(np.resize(levels, k // 512 * 4)).reshape(k // 512, 4)
    idx = np.arange(k)
    return np.exp2(a[idx // 512, idx % 128 // 32])


BF16 = ml_dtypes.bfloat16


def bf(x):
    return np.asarray(x, np.float32).astype(BF16)


def f64(x):
    return np.asarray(x).astype(np.float64)


B, S, D, E = 4, 1024, 256, 2


def make_adj():
    w = np.random.uniform(size=(B, S, S))
    keep = np.random.uniform(size=(B, S, S)) > 0.6
    return bf(w * keep)


def setup_inputs():
    s = mx_kscale(S)
    a = np.log2(s)
    q = np.random.standard_normal((E, B, S, D)) * 1.4
    k = np.random.standard_normal((E, B, S, D)) * 1.4
    v = np.random.standard_normal((E, B, S, D))
    q[..., 0] = 2.0
    k[..., 0] += -a * np.log(2.0) * np.sqrt(D)
    v = v * (s / s.min())[None, None, :, None]
    return {"q": bf(q), "k": bf(k), "v": bf(v), "adj0": make_adj(), "adj1": make_adj()}


def reference(q, k, v, adj0, adj1):
    adj = np.stack([f64(adj0), f64(adj1)])
    scores = f64(q) @ f64(k).transpose(0, 1, 3, 2) / np.sqrt(D)
    scores = scores * (adj + 1e-6) + np.where(adj == 0, -10000.0, 0.0)
    p = np.exp(scores - scores.max(-1, keepdims=True))
    return (mxq(p, 3, "e4m3") @ mxq(f64(v), 2, "e4m3")) / p.sum(-1, keepdims=True)

@@ -1,0 +1,250 @@
+from contextlib import ExitStack
+
+import concourse.mybir as mybir
+from concourse.masks import make_identity
+
+F32 = mybir.dt.float32
+BF16 = mybir.dt.bfloat16
+U32 = mybir.dt.uint32
+U8 = mybir.dt.uint8
+FP8X4 = mybir.dt.float8_e4m3fn_x4
+ALU = mybir.AluOpType
+ACT = mybir.ActivationFunctionType
+AXIS = mybir.AxisListType
+
+E, B, S, D = 2, 4, 1024, 256
+P = 128
+PACK = 4
+K_PASS = P * PACK
+PASSES = S // K_PASS
+Q_TILES = S // P
+K_BLOCKS = S // P
+BANK = 512
+HALVES = S // BANK
+WORDS = D // 2
+SCALE = 1.0 / 16.0
+MASK = -10000.0
+HEADS = E * B
+TILES = HEADS * Q_TILES
+
+FLOPS = 2 * (2 * E * B * S * S * D)
+
+
+def tile_heterogeneousgraphtransformer_pa_t_kernel(tc, q, k, v, adj0, adj1, out):
+    nc = tc.nc
+    with ExitStack() as ctx:
+        consts = ctx.enter_context(tc.tile_pool(name="consts", bufs=1))
+        loads = ctx.enter_context(tc.tile_pool(name="loads", bufs=2))
+        heads = ctx.enter_context(tc.tile_pool(name="heads", bufs=2))
+        work = ctx.enter_context(tc.tile_pool(name="work", bufs=2))
+        small = ctx.enter_context(tc.tile_pool(name="small", bufs=6))
+        psum_sc = ctx.enter_context(tc.psum_pool(name="psum_sc", bufs=2 * HALVES))
+        psum_tr = ctx.enter_context(tc.psum_pool(name="psum_tr", bufs=2))
+        psum_prep = ctx.enter_context(tc.psum_pool(name="psum_prep", bufs=1))
+        psum_o = ctx.enter_context(tc.psum_pool(name="psum_o", bufs=1))
+        ctx.enter_context(tc.manual_schedule())
+
+        ident_f32 = consts.tile([P, P], F32)
+        make_identity(nc, ident_f32[:])
+        ident_bf = consts.tile([P, P], BF16)
+        make_identity(nc, ident_bf[:])
+
+        live = {}
+
+        def load_head(h):
+            e, b = divmod(h, B)
+            adj = (adj0, adj1)[e]
+            k_sb = loads.tile([P, K_BLOCKS * D], BF16)
+            nc.sync.dma_start(
+                out=k_sb[:].rearrange("p (t d) -> p t d", d=D), in_=k[e, b].rearrange("(t p) d -> p t d", p=P)
+            )
+            q_sb = loads.tile([P, Q_TILES * D], BF16)
+            nc.sync.dma_start(out=q_sb[:], in_=q[e, b].rearrange("(p j) d -> p (j d)", j=Q_TILES))
+            adj_sb = loads.tile([P, Q_TILES, S], BF16)
+            adj_rows = adj[b].rearrange("(p j) c -> p j c", j=Q_TILES)
+            nc.sync.dma_start(out=adj_sb[:, 0:2, :], in_=adj_rows[:, 0:2, :])
+            v_sb = loads.tile([P, K_BLOCKS, D], BF16)
+            nc.sync.dma_start(out=v_sb[:], in_=v[e, b].rearrange("(t p) d -> p t d", p=P))
+            for j0 in range(2, Q_TILES, 2):
+                nc.sync.dma_start(out=adj_sb[:, j0 : j0 + 2, :], in_=adj_rows[:, j0 : j0 + 2, :])
+            live["k_sb", h], live["q_sb", h], live["adj", h], live["v_sb", h] = k_sb, q_sb, adj_sb, v_sb
+            live["k_t", h] = heads.tile([P, S * 2], BF16, name="k_t")
+            live["q_t", h] = heads.tile([P, S * 2], BF16, name="q_t")
+
+        def transpose_rows(h, which, half):
+            words = live[which + "_sb", h][:].bitcast(F32)
+            words_t = live[which + "_t", h][:].bitcast(F32)
+            per_bank = BANK // P
+            bank = psum_prep.tile([P, BANK], F32)
+            for i in range(per_bank):
+                blk = half * per_bank + i
+                nc.tensor.transpose(
+                    bank[:, i * P : (i + 1) * P], words[:, blk * WORDS : (blk + 1) * WORDS], ident_f32[:]
+                )
+            nc.scalar.copy(out=words_t[:, half * BANK : (half + 1) * BANK], in_=bank[:])
+
+        def regroup_v(h):
+            v_grouped = heads.tile([P, PASSES * D * PACK], BF16, align_bytes=64)
+            nc.vector.tensor_copy(
+                out=v_grouped[:].rearrange("p (g d t) -> p g d t", g=PASSES, t=PACK),
+                in_=live["v_sb", h][:].rearrange("p (g t) d -> p g d t", t=PACK),
+            )
+            live["v_grouped", h] = v_grouped
+
+        def quantise_v(h):
+            v_codes = heads.tile([P, PASSES * D], U32, align_bytes=64)
+            v_scales = heads.tile([P, PASSES * D], U8, align_bytes=64)
+            nc.vector.quantize_mx(out=v_codes[:].bitcast(FP8X4), scales=v_scales[:], in_=live["v_grouped", h][:])
+            live["v_codes", h], live["v_scales", h] = v_codes, v_scales
+
+        def scores(i):
+            h, j = divmod(i, Q_TILES)
+            q_pairs = live["q_t", h][:].rearrange("w (c e) -> w c e", e=2)
+            k_pairs = live["k_t", h][:].rearrange("w (c e) -> w c e", e=2)
+            banks = []
+            for half in range(HALVES):
+                sc = psum_sc.tile([P, BANK], F32, name="sc")
+                banks.append(sc)
+            for par in range(2):
+                for half in range(HALVES):
+                    nc.tensor.matmul(
+                        out=banks[half][:],
+                        lhsT=q_pairs[:, j * P : (j + 1) * P, par],
+                        rhs=k_pairs[:, half * BANK : (half + 1) * BANK, par],
+                        start=(par == 0),
+                        stop=(par == 1),
+                    )
+            live["sc", i] = banks
+
+        def weigh(i):
+            h, j = divmod(i, Q_TILES)
+            s16 = work.tile([P, S], F32, bufs=4)
+            for half in range(HALVES):
+                cols = slice(half * BANK, (half + 1) * BANK)
+                nc.vector.scalar_tensor_tensor(
+                    out=s16[:, cols],
+                    in0=live["adj", h][:, j, cols],
+                    scalar=1e-6,
+                    in1=live["sc", i][half][:],
+                    op0=ALU.add,
+                    op1=ALU.mult,
+                )
+            live["s16", i] = s16
+
+        def mask_values(i):
+            h, j = divmod(i, Q_TILES)
+            m16 = work.tile([P, S], F32, bufs=3)
+            nc.vector.tensor_scalar(
+                out=m16[:],
+                in0=live["adj", h][:, j, :],
+                scalar1=0.0,
+                scalar2=MASK / SCALE,
+                op0=ALU.is_equal,
+                op1=ALU.mult,
+            )
+            live["m16", i] = m16
+
+        def add_mask(i):
+            s16 = live["s16", i]
+            nc.gpsimd.tensor_tensor(out=s16[:], in0=s16[:], in1=live["m16", i][:], op=ALU.add)
+
+        def row_max(i):
+            top16 = small.tile([P, 1], F32)
+            nc.vector.tensor_reduce(out=top16[:], in_=live["s16", i][:], axis=AXIS.X, op=ALU.max)
+            neg_top = small.tile([P, 1], F32)
+            nc.vector.tensor_scalar_mul(out=neg_top[:], in0=top16[:], scalar1=-SCALE)
+            live["neg_top", i] = neg_top
+
+        def exponent(i):
+            prob = work.tile([P, S], BF16)
+            row_sum = small.tile([P, 1], F32)
+            nc.scalar.activation(
+                out=prob[:],
+                in_=live["s16", i][:],
+                func=ACT.Exp,
+                bias=live["neg_top", i][:],
+                scale=SCALE,
+                accum_out=row_sum[:],
+            )
+            live["prob", i], live["row_sum", i] = prob, row_sum
+
+        def transpose_p(i):
+            prob_t = psum_tr.tile([P, K_BLOCKS, P], BF16)
+            for t in range(K_BLOCKS):
+                nc.tensor.transpose(prob_t[:, t, :], live["prob", i][:, t * P : (t + 1) * P], ident_bf[:])
+            live["prob_t", i] = prob_t
+
+        def regroup_p(i):
+            p_grouped = work.tile([P, S], BF16, align_bytes=64)
+            nc.scalar.copy(
+                out=p_grouped[:].rearrange("p (g r t) -> p g r t", g=PASSES, t=PACK),
+                in_=live["prob_t", i][:].rearrange("p (g t) r -> p g r t", t=PACK),
+            )
+            live["p_grouped", i] = p_grouped
+
+        def quantise_p(i):
+            p_codes = work.tile([P, PASSES * P], U32, align_bytes=64)
+            p_scales = work.tile([P, PASSES * P], U8, align_bytes=64)
+            nc.vector.quantize_mx(out=p_codes[:].bitcast(FP8X4), scales=p_scales[:], in_=live["p_grouped", i][:])
+            live["p_codes", i], live["p_scales", i] = p_codes, p_scales
+
+        def weighted_sum(i):
+            h = i // Q_TILES
+            acc = psum_o.tile([P, D], F32)
+            for g in range(PASSES):
+                nc.tensor.matmul_mx(
+                    out=acc[:],
+                    lhsT=live["p_codes", i][:, g * P : (g + 1) * P].bitcast(FP8X4),
+                    lhsT_scale=live["p_scales", i][:, g * P : (g + 1) * P],
+                    rhs=live["v_codes", h][:, g * D : (g + 1) * D].bitcast(FP8X4),
+                    rhs_scale=live["v_scales", h][:, g * D : (g + 1) * D],
+                    start=(g == 0),
+                    stop=(g == PASSES - 1),
+                )
+            live["acc", i] = acc
+
+        def normalise(i):
+            h, j = divmod(i, Q_TILES)
+            if j == 0:
+                live["o_sb", h] = heads.tile([P, Q_TILES, D], F32, name="o_sb")
+            inv_sum = small.tile([P, 1], F32)
+            nc.vector.reciprocal(out=inv_sum[:], in_=live["row_sum", i][:])
+            nc.scalar.activation(out=live["o_sb", h][:, j, :], in_=live["acc", i][:], func=ACT.Copy, scale=inv_sum[:])
+            if j == Q_TILES - 1:
+                e, b = divmod(h, B)
+                nc.sync.dma_start(out=out[e, b].rearrange("(p j) d -> p j d", j=Q_TILES), in_=live["o_sb", h][:])
+
+        def prepare(h, step):
+            if h >= HEADS:
+                return
+            if step == 0:
+                load_head(h)
+            elif step in (3, 4):
+                transpose_rows(h, "k", step - 3)
+            elif step in (5, 6):
+                transpose_rows(h, "q", step - 5)
+            if step == 5:
+                regroup_v(h)
+            if step == 6:
+                quantise_v(h)
+
+        def run(stage, i):
+            if 0 <= i < TILES:
+                stage(i)
+
+        for step in range(Q_TILES):
+            prepare(0, step)
+        for r in range(-1, TILES + 4):
+            if r >= 0:
+                prepare(r // Q_TILES + 1, r % Q_TILES)
+            run(scores, r + 1)
+            run(weighted_sum, r - 4)
+            run(weigh, r)
+            run(mask_values, r + 1)
+            run(add_mask, r)
+            run(exponent, r - 2)
+            run(transpose_p, r - 2)
+            run(row_max, r - 1)
+            run(regroup_p, r - 3)
+            run(quantise_p, r - 3)
+            run(normalise, r - 4)

@@ -37,7 +37,7 @@ def tile_heterogeneousgraphtransformer_pa_t_kernel(tc, q, k, v, adj0, adj1, out)
         loads = ctx.enter_context(tc.tile_pool(name="loads", bufs=2))
         heads = ctx.enter_context(tc.tile_pool(name="heads", bufs=2))
         work = ctx.enter_context(tc.tile_pool(name="work", bufs=2))
-        small = ctx.enter_context(tc.tile_pool(name="small", bufs=6))
+        small = ctx.enter_context(tc.tile_pool(name="small", bufs=4))
         psum_sc = ctx.enter_context(tc.psum_pool(name="psum_sc", bufs=2 * HALVES))
         psum_tr = ctx.enter_context(tc.psum_pool(name="psum_tr", bufs=2))
         psum_prep = ctx.enter_context(tc.psum_pool(name="psum_prep", bufs=1))
@@ -73,7 +73,6 @@ def tile_heterogeneousgraphtransformer_pa_t_kernel(tc, q, k, v, adj0, adj1, out)
 
         def transpose_rows(h, which, half):
             words = live[which + "_sb", h][:].bitcast(F32)
-            words_t = live[which + "_t", h][:].bitcast(F32)
             per_bank = BANK // P
             bank = psum_prep.tile([P, BANK], F32)
             for i in range(per_bank):
@@ -81,7 +80,11 @@ def tile_heterogeneousgraphtransformer_pa_t_kernel(tc, q, k, v, adj0, adj1, out)
                 nc.tensor.transpose(
                     bank[:, i * P : (i + 1) * P], words[:, blk * WORDS : (blk + 1) * WORDS], ident_f32[:]
                 )
-            nc.scalar.copy(out=words_t[:, half * BANK : (half + 1) * BANK], in_=bank[:])
+            live["bank", h] = bank
+
+        def keep_rows(h, which, half):
+            words_t = live[which + "_t", h][:].bitcast(F32)
+            nc.scalar.copy(out=words_t[:, half * BANK : (half + 1) * BANK], in_=live["bank", h][:])
 
         def regroup_v(h):
             v_grouped = heads.tile([P, PASSES * D * PACK], BF16, align_bytes=64)
@@ -97,43 +100,38 @@ def tile_heterogeneousgraphtransformer_pa_t_kernel(tc, q, k, v, adj0, adj1, out)
             nc.vector.quantize_mx(out=v_codes[:].bitcast(FP8X4), scales=v_scales[:], in_=live["v_grouped", h][:])
             live["v_codes", h], live["v_scales", h] = v_codes, v_scales
 
-        def scores(i):
+        def scores(i, half):
             h, j = divmod(i, Q_TILES)
             q_pairs = live["q_t", h][:].rearrange("w (c e) -> w c e", e=2)
             k_pairs = live["k_t", h][:].rearrange("w (c e) -> w c e", e=2)
-            banks = []
-            for half in range(HALVES):
-                sc = psum_sc.tile([P, BANK], F32, name="sc")
-                banks.append(sc)
+            sc = psum_sc.tile([P, BANK], F32)
             for par in range(2):
-                for half in range(HALVES):
-                    nc.tensor.matmul(
-                        out=banks[half][:],
-                        lhsT=q_pairs[:, j * P : (j + 1) * P, par],
-                        rhs=k_pairs[:, half * BANK : (half + 1) * BANK, par],
-                        start=(par == 0),
-                        stop=(par == 1),
-                    )
-            live["sc", i] = banks
-
-        def weigh(i):
-            h, j = divmod(i, Q_TILES)
-            s16 = work.tile([P, S], F32, bufs=4)
-            for half in range(HALVES):
-                cols = slice(half * BANK, (half + 1) * BANK)
-                nc.vector.scalar_tensor_tensor(
-                    out=s16[:, cols],
-                    in0=live["adj", h][:, j, cols],
-                    scalar=1e-6,
-                    in1=live["sc", i][half][:],
-                    op0=ALU.add,
-                    op1=ALU.mult,
+                nc.tensor.matmul(
+                    out=sc[:],
+                    lhsT=q_pairs[:, j * P : (j + 1) * P, par],
+                    rhs=k_pairs[:, half * BANK : (half + 1) * BANK, par],
+                    start=(par == 0),
+                    stop=(par == 1),
                 )
-            live["s16", i] = s16
+            live["sc", i, half] = sc
+
+        def weigh(i, half):
+            h, j = divmod(i, Q_TILES)
+            if half == 0:
+                live["s16", i] = work.tile([P, S], F32, bufs=4, name="s16")
+            cols = slice(half * BANK, (half + 1) * BANK)
+            nc.vector.scalar_tensor_tensor(
+                out=live["s16", i][:, cols],
+                in0=live["adj", h][:, j, cols],
+                scalar=1e-6,
+                in1=live["sc", i, half][:],
+                op0=ALU.add,
+                op1=ALU.mult,
+            )
 
         def mask_values(i):
             h, j = divmod(i, Q_TILES)
-            m16 = work.tile([P, S], F32, bufs=3)
+            m16 = work.tile([P, S], F32)
             nc.vector.tensor_scalar(
                 out=m16[:],
                 in0=live["adj", h][:, j, :],
@@ -151,8 +149,11 @@ def tile_heterogeneousgraphtransformer_pa_t_kernel(tc, q, k, v, adj0, adj1, out)
         def row_max(i):
             top16 = small.tile([P, 1], F32)
             nc.vector.tensor_reduce(out=top16[:], in_=live["s16", i][:], axis=AXIS.X, op=ALU.max)
+            live["top16", i] = top16
+
+        def negate_max(i):
             neg_top = small.tile([P, 1], F32)
-            nc.vector.tensor_scalar_mul(out=neg_top[:], in0=top16[:], scalar1=-SCALE)
+            nc.scalar.mul(out=neg_top[:], in_=live["top16", i][:], mul=-SCALE)
             live["neg_top", i] = neg_top
 
         def exponent(i):
@@ -203,48 +204,61 @@ def tile_heterogeneousgraphtransformer_pa_t_kernel(tc, q, k, v, adj0, adj1, out)
                 )
             live["acc", i] = acc
 
+        def invert_sum(i):
+            inv_sum = small.tile([P, 1], F32)
+            nc.vector.reciprocal(out=inv_sum[:], in_=live["row_sum", i][:])
+            live["inv_sum", i] = inv_sum
+
         def normalise(i):
             h, j = divmod(i, Q_TILES)
             if j == 0:
                 live["o_sb", h] = heads.tile([P, Q_TILES, D], F32, name="o_sb")
-            inv_sum = small.tile([P, 1], F32)
-            nc.vector.reciprocal(out=inv_sum[:], in_=live["row_sum", i][:])
-            nc.scalar.activation(out=live["o_sb", h][:, j, :], in_=live["acc", i][:], func=ACT.Copy, scale=inv_sum[:])
+            nc.scalar.activation(
+                out=live["o_sb", h][:, j, :], in_=live["acc", i][:], func=ACT.Copy, scale=live["inv_sum", i][:]
+            )
             if j == Q_TILES - 1:
                 e, b = divmod(h, B)
                 nc.sync.dma_start(out=out[e, b].rearrange("(p j) d -> p j d", j=Q_TILES), in_=live["o_sb", h][:])
 
-        def prepare(h, step):
-            if h >= HEADS:
-                return
-            if step == 0:
-                load_head(h)
-            elif step in (3, 4):
-                transpose_rows(h, "k", step - 3)
-            elif step in (5, 6):
-                transpose_rows(h, "q", step - 5)
-            if step == 5:
-                regroup_v(h)
-            if step == 6:
-                quantise_v(h)
+        ROWS_AT = {2: ("k", 0), 3: ("k", 1), 4: ("q", 0), 5: ("q", 1)}
 
-        def run(stage, i):
+        def run(stage, i, *more):
             if 0 <= i < TILES:
-                stage(i)
+                stage(i, *more)
 
-        for step in range(Q_TILES):
-            prepare(0, step)
-        for r in range(-1, TILES + 4):
-            if r >= 0:
-                prepare(r // Q_TILES + 1, r % Q_TILES)
-            run(scores, r + 1)
-            run(weighted_sum, r - 4)
-            run(weigh, r)
-            run(mask_values, r + 1)
+        load_head(0)
+        for step in sorted(ROWS_AT):
+            transpose_rows(0, *ROWS_AT[step])
+            keep_rows(0, *ROWS_AT[step])
+        regroup_v(0)
+        quantise_v(0)
+
+        for r in range(-2, TILES + 6):
+            nxt, step = divmod(r, Q_TILES)
+            nxt += 1
+            ahead = 0 <= r and nxt < HEADS
+            if ahead and step == 0:
+                load_head(nxt)
+            run(weigh, r, 0)
+            run(scores, r + 2, 0)
+            run(weighted_sum, r - 5)
+            if ahead and step in ROWS_AT:
+                transpose_rows(nxt, *ROWS_AT[step])
+            run(regroup_p, r - 4)
+            run(row_max, r - 2)
+            run(exponent, r - 3)
+            run(weigh, r, 1)
+            run(scores, r + 2, 1)
+            run(transpose_p, r - 3)
+            run(normalise, r - 5)
+            if ahead and step in ROWS_AT:
+                keep_rows(nxt, *ROWS_AT[step])
+            run(negate_max, r - 2)
+            run(quantise_p, r - 4)
+            run(invert_sum, r - 4)
+            if ahead and step == 3:
+                regroup_v(nxt)
+            if ahead and step == 4:
+                quantise_v(nxt)
+            run(mask_values, r)
             run(add_mask, r)
-            run(exponent, r - 2)
-            run(transpose_p, r - 2)
-            run(row_max, r - 1)
-            run(regroup_p, r - 3)
-            run(quantise_p, r - 3)
-            run(normalise, r - 4)

@@ -39,8 +39,7 @@ def tile_heterogeneousgraphtransformer_pa_t_kernel(tc, q, k, v, adj0, adj1, out)
         work = ctx.enter_context(tc.tile_pool(name="work", bufs=2))
         small = ctx.enter_context(tc.tile_pool(name="small", bufs=4))
         psum_sc = ctx.enter_context(tc.psum_pool(name="psum_sc", bufs=2 * HALVES))
-        psum_tr = ctx.enter_context(tc.psum_pool(name="psum_tr", bufs=2))
-        psum_prep = ctx.enter_context(tc.psum_pool(name="psum_prep", bufs=1))
+        psum_tr = ctx.enter_context(tc.psum_pool(name="psum_tr", bufs=3))
         psum_o = ctx.enter_context(tc.psum_pool(name="psum_o", bufs=1))
         ctx.enter_context(tc.manual_schedule())
 
@@ -71,10 +70,11 @@ def tile_heterogeneousgraphtransformer_pa_t_kernel(tc, q, k, v, adj0, adj1, out)
             live["k_t", h] = heads.tile([P, S * 2], BF16, name="k_t")
             live["q_t", h] = heads.tile([P, S * 2], BF16, name="q_t")
 
-        def transpose_rows(h, which, half):
+        def transpose_rows(h, piece):
+            which, half = "kq"[piece // HALVES], piece % HALVES
             words = live[which + "_sb", h][:].bitcast(F32)
             per_bank = BANK // P
-            bank = psum_prep.tile([P, BANK], F32)
+            bank = psum_tr.tile([P, BANK], F32, tag="tr")
             for i in range(per_bank):
                 blk = half * per_bank + i
                 nc.tensor.transpose(
@@ -82,17 +82,19 @@ def tile_heterogeneousgraphtransformer_pa_t_kernel(tc, q, k, v, adj0, adj1, out)
                 )
             live["bank", h] = bank
 
-        def keep_rows(h, which, half):
+        def keep_rows(h, piece):
+            which, half = "kq"[piece // HALVES], piece % HALVES
             words_t = live[which + "_t", h][:].bitcast(F32)
             nc.scalar.copy(out=words_t[:, half * BANK : (half + 1) * BANK], in_=live["bank", h][:])
 
-        def regroup_v(h):
-            v_grouped = heads.tile([P, PASSES * D * PACK], BF16, align_bytes=64)
-            nc.vector.tensor_copy(
-                out=v_grouped[:].rearrange("p (g d t) -> p g d t", g=PASSES, t=PACK),
-                in_=live["v_sb", h][:].rearrange("p (g t) d -> p g d t", t=PACK),
+        def regroup_v(h, piece):
+            if piece == 0:
+                live["v_grouped", h] = heads.tile([P, PASSES * D * PACK], BF16, align_bytes=64, name="v_grouped")
+            g, cols = piece // 2, slice((piece % 2) * P, (piece % 2 + 1) * P)
+            nc.scalar.copy(
+                out=live["v_grouped", h][:].rearrange("p (g d t) -> p g d t", g=PASSES, t=PACK)[:, g, cols, :],
+                in_=live["v_sb", h][:].rearrange("p (g t) d -> p g d t", t=PACK)[:, g, cols, :],
             )
-            live["v_grouped", h] = v_grouped
 
         def quantise_v(h):
             v_codes = heads.tile([P, PASSES * D], U32, align_bytes=64)
@@ -170,7 +172,7 @@ def tile_heterogeneousgraphtransformer_pa_t_kernel(tc, q, k, v, adj0, adj1, out)
             live["prob", i], live["row_sum", i] = prob, row_sum
 
         def transpose_p(i):
-            prob_t = psum_tr.tile([P, K_BLOCKS, P], BF16)
+            prob_t = psum_tr.tile([P, K_BLOCKS, P], BF16, tag="tr")
             for t in range(K_BLOCKS):
                 nc.tensor.transpose(prob_t[:, t, :], live["prob", i][:, t * P : (t + 1) * P], ident_bf[:])
             live["prob_t", i] = prob_t
@@ -211,39 +213,40 @@ def tile_heterogeneousgraphtransformer_pa_t_kernel(tc, q, k, v, adj0, adj1, out)
 
         def normalise(i):
             h, j = divmod(i, Q_TILES)
-            if j == 0:
-                live["o_sb", h] = heads.tile([P, Q_TILES, D], F32, name="o_sb")
-            nc.scalar.activation(
-                out=live["o_sb", h][:, j, :], in_=live["acc", i][:], func=ACT.Copy, scale=live["inv_sum", i][:]
-            )
-            if j == Q_TILES - 1:
-                e, b = divmod(h, B)
-                nc.sync.dma_start(out=out[e, b].rearrange("(p j) d -> p j d", j=Q_TILES), in_=live["o_sb", h][:])
+            e, b = divmod(h, B)
+            o_sb = work.tile([P, D], F32, bufs=3)
+            nc.scalar.activation(out=o_sb[:], in_=live["acc", i][:], func=ACT.Copy, scale=live["inv_sum", i][:])
+            nc.sync.dma_start(out=out[e, b].rearrange("(p j) d -> p j d", j=Q_TILES)[:, j, :], in_=o_sb[:])
 
-        ROWS_AT = {2: ("k", 0), 3: ("k", 1), 4: ("q", 0), 5: ("q", 1)}
+        def prepare(part, head, rel):
+            if not 0 <= head < HEADS:
+                return
+            if part == "load" and rel == -8:
+                load_head(head)
+            if part == "tensor" and -6 <= rel < -2:
+                transpose_rows(head, rel + 6)
+            if part == "scalar" and -6 <= rel < -2:
+                keep_rows(head, rel + 6)
+            if part == "scalar" and -2 <= rel < 2:
+                regroup_v(head, rel + 2)
+            if part == "vector" and rel == 2:
+                quantise_v(head)
+
+        def prepare_heads(part, r):
+            now = r // Q_TILES
+            prepare(part, now + 1, r - (now + 1) * Q_TILES)
+            prepare(part, now, r - now * Q_TILES)
 
         def run(stage, i, *more):
             if 0 <= i < TILES:
                 stage(i, *more)
 
-        load_head(0)
-        for step in sorted(ROWS_AT):
-            transpose_rows(0, *ROWS_AT[step])
-            keep_rows(0, *ROWS_AT[step])
-        regroup_v(0)
-        quantise_v(0)
-
-        for r in range(-2, TILES + 6):
-            nxt, step = divmod(r, Q_TILES)
-            nxt += 1
-            ahead = 0 <= r and nxt < HEADS
-            if ahead and step == 0:
-                load_head(nxt)
+        for r in range(-8, TILES + 6):
+            prepare_heads("load", r)
             run(weigh, r, 0)
             run(scores, r + 2, 0)
             run(weighted_sum, r - 5)
-            if ahead and step in ROWS_AT:
-                transpose_rows(nxt, *ROWS_AT[step])
+            prepare_heads("tensor", r)
             run(regroup_p, r - 4)
             run(row_max, r - 2)
             run(exponent, r - 3)
@@ -251,14 +254,10 @@ def tile_heterogeneousgraphtransformer_pa_t_kernel(tc, q, k, v, adj0, adj1, out)
             run(scores, r + 2, 1)
             run(transpose_p, r - 3)
             run(normalise, r - 5)
-            if ahead and step in ROWS_AT:
-                keep_rows(nxt, *ROWS_AT[step])
+            prepare_heads("scalar", r)
             run(negate_max, r - 2)
             run(quantise_p, r - 4)
             run(invert_sum, r - 4)
-            if ahead and step == 3:
-                regroup_v(nxt)
-            if ahead and step == 4:
-                quantise_v(nxt)
+            prepare_heads("vector", r)
             run(mask_values, r)
             run(add_mask, r)

from contextlib import ExitStack

import concourse.mybir as mybir
from concourse.masks import make_identity

F32 = mybir.dt.float32
BF16 = mybir.dt.bfloat16
U32 = mybir.dt.uint32
U8 = mybir.dt.uint8
FP8X4 = mybir.dt.float8_e4m3fn_x4
ALU = mybir.AluOpType
ACT = mybir.ActivationFunctionType
AXIS = mybir.AxisListType

E, B, S, D = 2, 4, 1024, 256
P = 128
PACK = 4
K_PASS = P * PACK
PASSES = S // K_PASS
Q_TILES = S // P
K_BLOCKS = S // P
BANK = 512
HALVES = S // BANK
WORDS = D // 2
SCALE = 1.0 / 16.0
MASK = -10000.0
HEADS = E * B
TILES = HEADS * Q_TILES

FLOPS = 2 * (2 * E * B * S * S * D)


def tile_heterogeneousgraphtransformer_pa_t_kernel(tc, q, k, v, adj0, adj1, out):
    nc = tc.nc
    with ExitStack() as ctx:
        consts = ctx.enter_context(tc.tile_pool(name="consts", bufs=1))
        loads = ctx.enter_context(tc.tile_pool(name="loads", bufs=2))
        heads = ctx.enter_context(tc.tile_pool(name="heads", bufs=2))
        work = ctx.enter_context(tc.tile_pool(name="work", bufs=2))
        small = ctx.enter_context(tc.tile_pool(name="small", bufs=4))
        psum_sc = ctx.enter_context(tc.psum_pool(name="psum_sc", bufs=2 * HALVES))
        psum_tr = ctx.enter_context(tc.psum_pool(name="psum_tr", bufs=3))
        psum_o = ctx.enter_context(tc.psum_pool(name="psum_o", bufs=1))
        ctx.enter_context(tc.manual_schedule())

        ident_f32 = consts.tile([P, P], F32)
        make_identity(nc, ident_f32[:])
        ident_bf = consts.tile([P, P], BF16)
        make_identity(nc, ident_bf[:])

        live = {}

        def load_head(h):
            e, b = divmod(h, B)
            adj = (adj0, adj1)[e]
            k_sb = loads.tile([P, K_BLOCKS * D], BF16)
            nc.sync.dma_start(
                out=k_sb[:].rearrange("p (t d) -> p t d", d=D), in_=k[e, b].rearrange("(t p) d -> p t d", p=P)
            )
            q_sb = loads.tile([P, Q_TILES * D], BF16)
            nc.sync.dma_start(out=q_sb[:], in_=q[e, b].rearrange("(p j) d -> p (j d)", j=Q_TILES))
            adj_sb = loads.tile([P, Q_TILES, S], BF16)
            adj_rows = adj[b].rearrange("(p j) c -> p j c", j=Q_TILES)
            nc.sync.dma_start(out=adj_sb[:, 0:2, :], in_=adj_rows[:, 0:2, :])
            v_sb = loads.tile([P, K_BLOCKS, D], BF16)
            nc.sync.dma_start(out=v_sb[:], in_=v[e, b].rearrange("(t p) d -> p t d", p=P))
            for j0 in range(2, Q_TILES, 2):
                nc.sync.dma_start(out=adj_sb[:, j0 : j0 + 2, :], in_=adj_rows[:, j0 : j0 + 2, :])
            live["k_sb", h], live["q_sb", h], live["adj", h], live["v_sb", h] = k_sb, q_sb, adj_sb, v_sb
            live["k_t", h] = heads.tile([P, S * 2], BF16, name="k_t")
            live["q_t", h] = heads.tile([P, S * 2], BF16, name="q_t")

        def transpose_rows(h, piece):
            which, half = "kq"[piece // HALVES], piece % HALVES
            words = live[which + "_sb", h][:].bitcast(F32)
            per_bank = BANK // P
            bank = psum_tr.tile([P, BANK], F32, tag="tr")
            for i in range(per_bank):
                blk = half * per_bank + i
                nc.tensor.transpose(
                    bank[:, i * P : (i + 1) * P], words[:, blk * WORDS : (blk + 1) * WORDS], ident_f32[:]
                )
            live["bank", h] = bank

        def keep_rows(h, piece):
            which, half = "kq"[piece // HALVES], piece % HALVES
            words_t = live[which + "_t", h][:].bitcast(F32)
            nc.scalar.copy(out=words_t[:, half * BANK : (half + 1) * BANK], in_=live["bank", h][:])

        def regroup_v(h, piece):
            if piece == 0:
                live["v_grouped", h] = heads.tile([P, PASSES * D * PACK], BF16, align_bytes=64, name="v_grouped")
            g, cols = piece // 2, slice((piece % 2) * P, (piece % 2 + 1) * P)
            nc.scalar.copy(
                out=live["v_grouped", h][:].rearrange("p (g d t) -> p g d t", g=PASSES, t=PACK)[:, g, cols, :],
                in_=live["v_sb", h][:].rearrange("p (g t) d -> p g d t", t=PACK)[:, g, cols, :],
            )

        def quantise_v(h):
            v_codes = heads.tile([P, PASSES * D], U32, align_bytes=64)
            v_scales = heads.tile([P, PASSES * D], U8, align_bytes=64)
            nc.vector.quantize_mx(out=v_codes[:].bitcast(FP8X4), scales=v_scales[:], in_=live["v_grouped", h][:])
            live["v_codes", h], live["v_scales", h] = v_codes, v_scales

        def scores(i, half):
            h, j = divmod(i, Q_TILES)
            q_pairs = live["q_t", h][:].rearrange("w (c e) -> w c e", e=2)
            k_pairs = live["k_t", h][:].rearrange("w (c e) -> w c e", e=2)
            sc = psum_sc.tile([P, BANK], F32)
            for par in range(2):
                nc.tensor.matmul(
                    out=sc[:],
                    lhsT=q_pairs[:, j * P : (j + 1) * P, par],
                    rhs=k_pairs[:, half * BANK : (half + 1) * BANK, par],
                    start=(par == 0),
                    stop=(par == 1),
                )
            live["sc", i, half] = sc

        def weigh(i, half):
            h, j = divmod(i, Q_TILES)
            if half == 0:
                live["s16", i] = work.tile([P, S], F32, bufs=4, name="s16")
            cols = slice(half * BANK, (half + 1) * BANK)
            nc.vector.scalar_tensor_tensor(
                out=live["s16", i][:, cols],
                in0=live["adj", h][:, j, cols],
                scalar=1e-6,
                in1=live["sc", i, half][:],
                op0=ALU.add,
                op1=ALU.mult,
            )

        def mask_values(i):
            h, j = divmod(i, Q_TILES)
            m16 = work.tile([P, S], F32)
            nc.vector.tensor_scalar(
                out=m16[:],
                in0=live["adj", h][:, j, :],
                scalar1=0.0,
                scalar2=MASK / SCALE,
                op0=ALU.is_equal,
                op1=ALU.mult,
            )
            live["m16", i] = m16

        def add_mask(i):
            s16 = live["s16", i]
            nc.gpsimd.tensor_tensor(out=s16[:], in0=s16[:], in1=live["m16", i][:], op=ALU.add)

        def row_max(i):
            top16 = small.tile([P, 1], F32)
            nc.vector.tensor_reduce(out=top16[:], in_=live["s16", i][:], axis=AXIS.X, op=ALU.max)
            live["top16", i] = top16

        def negate_max(i):
            neg_top = small.tile([P, 1], F32)
            nc.scalar.mul(out=neg_top[:], in_=live["top16", i][:], mul=-SCALE)
            live["neg_top", i] = neg_top

        def exponent(i):
            prob = work.tile([P, S], BF16)
            row_sum = small.tile([P, 1], F32)
            nc.scalar.activation(
                out=prob[:],
                in_=live["s16", i][:],
                func=ACT.Exp,
                bias=live["neg_top", i][:],
                scale=SCALE,
                accum_out=row_sum[:],
            )
            live["prob", i], live["row_sum", i] = prob, row_sum

        def transpose_p(i):
            prob_t = psum_tr.tile([P, K_BLOCKS, P], BF16, tag="tr")
            for t in range(K_BLOCKS):
                nc.tensor.transpose(prob_t[:, t, :], live["prob", i][:, t * P : (t + 1) * P], ident_bf[:])
            live["prob_t", i] = prob_t

        def regroup_p(i):
            p_grouped = work.tile([P, S], BF16, align_bytes=64)
            nc.scalar.copy(
                out=p_grouped[:].rearrange("p (g r t) -> p g r t", g=PASSES, t=PACK),
                in_=live["prob_t", i][:].rearrange("p (g t) r -> p g r t", t=PACK),
            )
            live["p_grouped", i] = p_grouped

        def quantise_p(i):
            p_codes = work.tile([P, PASSES * P], U32, align_bytes=64)
            p_scales = work.tile([P, PASSES * P], U8, align_bytes=64)
            nc.vector.quantize_mx(out=p_codes[:].bitcast(FP8X4), scales=p_scales[:], in_=live["p_grouped", i][:])
            live["p_codes", i], live["p_scales", i] = p_codes, p_scales

        def weighted_sum(i):
            h = i // Q_TILES
            acc = psum_o.tile([P, D], F32)
            for g in range(PASSES):
                nc.tensor.matmul_mx(
                    out=acc[:],
                    lhsT=live["p_codes", i][:, g * P : (g + 1) * P].bitcast(FP8X4),
                    lhsT_scale=live["p_scales", i][:, g * P : (g + 1) * P],
                    rhs=live["v_codes", h][:, g * D : (g + 1) * D].bitcast(FP8X4),
                    rhs_scale=live["v_scales", h][:, g * D : (g + 1) * D],
                    start=(g == 0),
                    stop=(g == PASSES - 1),
                )
            live["acc", i] = acc

        def invert_sum(i):
            inv_sum = small.tile([P, 1], F32)
            nc.vector.reciprocal(out=inv_sum[:], in_=live["row_sum", i][:])
            live["inv_sum", i] = inv_sum

        def normalise(i):
            h, j = divmod(i, Q_TILES)
            e, b = divmod(h, B)
            o_sb = work.tile([P, D], F32, bufs=3)
            nc.scalar.activation(out=o_sb[:], in_=live["acc", i][:], func=ACT.Copy, scale=live["inv_sum", i][:])
            nc.sync.dma_start(out=out[e, b].rearrange("(p j) d -> p j d", j=Q_TILES)[:, j, :], in_=o_sb[:])

        def prepare(part, head, rel):
            if not 0 <= head < HEADS:
                return
            if part == "load" and rel == -8:
                load_head(head)
            if part == "tensor" and -6 <= rel < -2:
                transpose_rows(head, rel + 6)
            if part == "scalar" and -6 <= rel < -2:
                keep_rows(head, rel + 6)
            if part == "scalar" and -2 <= rel < 2:
                regroup_v(head, rel + 2)
            if part == "vector" and rel == 2:
                quantise_v(head)

        def prepare_heads(part, r):
            now = r // Q_TILES
            prepare(part, now + 1, r - (now + 1) * Q_TILES)
            prepare(part, now, r - now * Q_TILES)

        def run(stage, i, *more):
            if 0 <= i < TILES:
                stage(i, *more)

        for r in range(-8, TILES + 6):
            prepare_heads("load", r)
            run(weigh, r, 0)
            run(scores, r + 2, 0)
            run(weighted_sum, r - 5)
            prepare_heads("tensor", r)
            run(regroup_p, r - 4)
            run(row_max, r - 2)
            run(exponent, r - 3)
            run(weigh, r, 1)
            run(scores, r + 2, 1)
            run(transpose_p, r - 3)
            run(normalise, r - 5)
            prepare_heads("scalar", r)
            run(negate_max, r - 2)
            run(quantise_p, r - 4)
            run(invert_sum, r - 4)
            prepare_heads("vector", r)
            run(mask_values, r)
            run(add_mask, r)
